import numpy as np
import ml_dtypes


def mxq(x, axis, fmt="e4m3"):
    dtype, down = {"e4m3": (ml_dtypes.float8_e4m3fn, 7), "e5m2": (ml_dtypes.float8_e5m2, 14)}[fmt]
    v = np.moveaxis(np.asarray(x, np.float32).astype(ml_dtypes.bfloat16).astype(np.float64), axis, -1)
    blocks = v.reshape(v.shape[:-1] + (-1, 32))
    amax = np.abs(blocks).max(-1, keepdims=True)
    byte = np.maximum(np.where(amax > 0, np.frexp(amax)[1] - 1 + 127, 0) - down, 1)
    scale = np.exp2(byte - 127.0)
    codes = (blocks / scale).astype(np.float32).astype(dtype).astype(np.float64)
    return np.moveaxis((codes * scale).reshape(v.shape), -1, axis)


WIDE = False


def mx_kscale(k):
    if not WIDE:
        return np.ones(k)
    levels = np.array([10, -10, 5, -5, 0])
    if k % 512:
        return np.exp2(np.random.permutation(np.resize(levels, k // 32))).repeat(32)
    a = np.empty((k // 512, 16))
    for p in range(k // 512):
        a[p, :8] = np.random.permutation(np.resize(levels, 8))
        for g in range(8):
            far = levels[np.abs(levels - a[p, g]) >= 10]
            a[p, g + 8] = far[np.random.randint(len(far))]
    return np.exp2(a.ravel()).repeat(32)


BF16 = ml_dtypes.bfloat16


def bf(x):
    return np.asarray(x, np.float32).astype(BF16)


def f64(x):
    return np.asarray(x).astype(np.float64)


B, F, C, N = 2048, 4, 512, 128
DIAG = 3.0 * np.log(C)
LAM = 3.0
TANH_RMS = 0.628
NH = N // 2
X0 = 5.0


def setup_inputs():
    t = mx_kscale(C)
    wide = float(t.max() > 1.0)
    x = np.random.standard_normal((B, F, N)) * LAM / np.sqrt(DIAG)
    p = np.tanh(np.random.standard_normal((F, C, N))) * np.sqrt(DIAG / N) / TANH_RMS
    x[:, :, 0] += wide * (X0 - x[:, :, 0])
    x[:, :, NH:] /= t.max() ** 2
    p[:, :, 0] -= np.log(t) / X0
    p[:, :, NH:] *= t[:, None]
    return {"x": bf(x), "patterns": bf(p)}


def reference(x, patterns):
    xt = f64(x).transpose(1, 0, 2)
    p = f64(patterns)
    gram = p @ p.transpose(0, 2, 1)
    s = xt @ p.transpose(0, 2, 1)
    e = np.exp(s - s.max(-1, keepdims=True))
    y = (mxq(e, 2, "e4m3") @ mxq(gram.transpose(0, 2, 1), 1, "e4m3")) / e.sum(-1, keepdims=True)
    return y.transpose(1, 0, 2)

@@ -1,0 +1,287 @@
+from contextlib import ExitStack
+
+import concourse.mybir as mybir
+from concourse.masks import make_identity
+
+F32 = mybir.dt.float32
+BF16 = mybir.dt.bfloat16
+U32 = mybir.dt.uint32
+U8 = mybir.dt.uint8
+FP8X4 = mybir.dt.float8_e4m3fn_x4
+ACT = mybir.ActivationFunctionType
+ALU = mybir.AluOpType
+AX = mybir.AxisListType
+
+P = 128
+B, F, C, N = 2048, 4, 512, 128
+T = C // P
+PB = P // T
+NB = B // P
+NT = NB * F
+NQ = NT // 2
+NG = F * T
+LAG = 6
+HELP = 8
+WARM = 5
+LENT = 4
+FLOPS = 2 * (B * F * C * N + F * C * C * N + B * F * C * C)
+
+
+def tile_hopfieldlayer_pa_t_kernel(tc, x, patterns, out):
+    nc = tc.nc
+    with ExitStack() as ctx:
+        ctx.enter_context(tc.manual_schedule())
+        keep = ctx.enter_context(tc.tile_pool(name="keep", bufs=1))
+        work = ctx.enter_context(tc.tile_pool(name="work", bufs=3))
+        small = ctx.enter_context(tc.tile_pool(name="small", bufs=6))
+        results = ctx.enter_context(tc.tile_pool(name="results", bufs=4))
+        logit_banks = ctx.enter_context(tc.psum_pool(name="logit_banks", bufs=LENT))
+        flip_banks = ctx.enter_context(tc.psum_pool(name="flip_banks", bufs=2))
+        product_banks = ctx.enter_context(tc.psum_pool(name="product_banks", bufs=2))
+
+        x_v = x.rearrange("(p i) f n -> p i (f n)", i=NB)
+        p_v = patterns.rearrange("f (p t) n -> p f t n", t=T)
+        out_v = out.rearrange("(p i) f c -> p i f c", i=NB)
+
+        p_sb = keep.tile([P, F, T, N], BF16)
+        x_sb = keep.tile([P, NB, F * N], BF16)
+        nc.sync.dma_start(out=p_sb[:, 0:2], in_=p_v[:, 0:2])
+        nc.sync.dma_start(out=x_sb[:, 0:2, :], in_=x_v[:, 0:2, :])
+        nc.sync.dma_start(out=p_sb[:, 2:4], in_=p_v[:, 2:4])
+        nc.sync.dma_start(out=x_sb[:, 2:4, :], in_=x_v[:, 2:4, :])
+        for i0 in (4, 8, 12):
+            nc.sync.dma_start(out=x_sb[:, i0 : i0 + 4, :], in_=x_v[:, i0 : i0 + 4, :])
+
+        ident = keep.tile([P, P], BF16)
+        make_identity(nc, ident[:])
+        one_column = keep.tile([P, 1], F32)
+        unused = keep.tile([P, 1], F32)
+        nc.vector.memset(one_column[:], 0.0)
+        nc.scalar.activation(out=unused[:], in_=one_column[:], func=ACT.Exp)
+        zeros = keep.tile([P, C], BF16)
+        nc.vector.memset(zeros[:], 0.0)
+        idle = logit_banks.tile([P, C], F32, tag="bank", name="idle")
+        for r in range(WARM):
+            nc.tensor.matmul(out=idle[:], lhsT=zeros[:, 0:P], rhs=zeros[:], start=True, stop=True)
+
+        pt = keep.tile([P, F, C], BF16)
+        xt = keep.tile([P, NB, F, P], BF16)
+        gram_words = keep.tile([P, F, C], U32, align_bytes=64)
+        gram_scales = keep.tile([P, F, C], U8, align_bytes=64)
+
+        def flip(blocks):
+            bank = flip_banks.tile([P, 2 * T, P], BF16, tag="bank", name="flipped")
+            for r in range(2 * T):
+                nc.tensor.transpose(out=bank[:, r, :], in_=blocks(r), identity=ident[:])
+            return bank
+
+        xt_ps, s_ps, neg_max, sums, e_sb, et_ps, et_sb, grouped = {}, {}, {}, {}, {}, {}, {}, {}
+        words, scales, inv_sums, y_ps, o_sb, gram_grouped = {}, {}, {}, {}, {}, {}
+
+        def flip_x(h):
+            xt_ps[h] = flip(lambda r: x_sb[:, 2 * h + r // F, (r % F) * N : (r % F + 1) * N])
+
+        def unload_x(h, on_vector):
+            dst = xt[:, 2 * h : 2 * h + 2].rearrange("n i f p -> n (i f) p")
+            if on_vector:
+                nc.vector.tensor_copy(out=dst, in_=xt_ps[h][:])
+            else:
+                nc.scalar.copy(out=dst, in_=xt_ps[h][:])
+
+        def flip_patterns(h):
+            bank = flip(lambda r: p_sb[:, 2 * h + r // T, r % T, :])
+            nc.vector.tensor_copy(out=pt[:, 2 * h : 2 * h + 2, :].rearrange("n f (t p) -> n (f t) p", p=P), in_=bank[:])
+
+        def logits(m):
+            s_ps[m] = logit_banks.tile([P, C], F32, tag="bank", name="s")
+            nc.tensor.matmul(out=s_ps[m][:], lhsT=xt[:, m // F, m % F, :], rhs=pt[:, m % F, :], start=True, stop=True)
+
+        def negated_max(m):
+            q, j = m // 2, m % 2
+            if j == 0:
+                neg_max[q] = small.tile([P, 2], F32, tag="neg_max", name="neg_max")
+            nc.vector.tensor_reduce(out=neg_max[q][:, j : j + 1], in_=s_ps[m][:], axis=AX.X, op=ALU.max, negate=True)
+
+        def exponentials(m):
+            q, j = m // 2, m % 2
+            if j == 0:
+                e_sb[q] = work.tile([P, 2 * T, P], BF16, tag="e", name="e")
+            if m % F == 0:
+                sums[m // F] = small.tile([P, F], F32, tag="sums", name="sums")
+            nc.scalar.activation(
+                out=e_sb[q][:, j * T : (j + 1) * T, :].rearrange("b t p -> b (t p)"),
+                in_=s_ps[m][:],
+                func=ACT.Exp,
+                bias=neg_max[q][:, j : j + 1],
+                scale=1.0,
+                accum_out=sums[m // F][:, m % F : m % F + 1],
+            )
+
+        def flip_pair(q):
+            et_ps[q] = flip(lambda r: e_sb[q][:, r, :])
+
+        def unload_pair(q):
+            if q < NQ - 1:
+                et_sb[q] = work.tile([P, 2 * T, P], BF16, tag="et", name="et", bufs=2)
+                nc.vector.tensor_copy(out=et_sb[q][:], in_=et_ps[q][:])
+
+        def regroup_pair(q):
+            i, f0 = q // 2, 2 * (q % 2)
+            if f0 == 0:
+                grouped[i] = work.tile([P, F, P, T], BF16, tag="grouped", name="grouped", align_bytes=64, bufs=1)
+            dst = grouped[i][:, f0 : f0 + 2]
+            if q < NQ - 1:
+                nc.gpsimd.tensor_scalar(
+                    out=dst,
+                    in0=et_sb[q][:].rearrange("p (j t) b -> p j b t", t=T),
+                    scalar1=1.0,
+                    scalar2=0.0,
+                    op0=ALU.mult,
+                    op1=ALU.add,
+                )
+            else:
+                nc.vector.tensor_copy(out=dst, in_=et_ps[q][:].rearrange("p (j t) b -> p j b t", t=T))
+
+        def quantise_group(i):
+            words[i] = work.tile([P, F * P], U32, tag="words", name="words", align_bytes=64)
+            scales[i] = work.tile([P, F * P], U8, tag="scales", name="scales", align_bytes=64)
+            nc.vector.quantize_mx(
+                out=words[i][:].bitcast(FP8X4),
+                scales=scales[i][:],
+                in_=grouped[i][:].rearrange("p f b t -> p (f b t)"),
+            )
+            inv_sums[i] = small.tile([P, F], F32, tag="inv_sums", name="inv_sums")
+            nc.vector.reciprocal(out=inv_sums[i][:], in_=sums[i][:])
+
+        def product(m):
+            if m < LENT - NG or m >= NT - 2 * LAG + 2:
+                y_ps[m] = logit_banks.tile([P, C], F32, tag="bank", name="y")
+            else:
+                y_ps[m] = product_banks.tile([P, C], F32, tag="bank", name="y")
+            if m >= 0:
+                i, f = m // F, m % F
+                nc.tensor.matmul_mx(
+                    out=y_ps[m][:],
+                    lhsT=words[i][:, f * P : (f + 1) * P].bitcast(FP8X4),
+                    lhsT_scale=scales[i][:, f * P : (f + 1) * P],
+                    rhs=gram_words[:, f, :].bitcast(FP8X4),
+                    rhs_scale=gram_scales[:, f, :],
+                    start=True,
+                    stop=True,
+                )
+            else:
+                f, cb = (m + NG) // T, (m + NG) % T
+                columns = pt[:, f, :].rearrange("n (s m) -> n s m", s=T)[:, :, cb * PB : (cb + 1) * PB]
+                for t in range(T):
+                    nc.tensor.matmul(
+                        out=y_ps[m][:, t * P : (t + 1) * P].rearrange("p (s m) -> p s m", s=T),
+                        lhsT=pt[:, f, t * P : (t + 1) * P],
+                        rhs=columns,
+                        start=True,
+                        stop=True,
+                    )
+
+        issued = [-NG]
+
+        def products(n):
+            for r in range(n):
+                if issued[0] < NT:
+                    product(issued[0])
+                    issued[0] += 1
+
+        def leave(m, on_vector):
+            if m >= 0:
+                q, j = m // 2, m % 2
+                if j == 0:
+                    o_sb[q] = results.tile([P, 2, C], F32, tag="o", name="o")
+                dst, src, factor = o_sb[q][:, j, :], y_ps[m][:], inv_sums[m // F][:, m % F : m % F + 1]
+                if on_vector:
+                    nc.vector.tensor_scalar_mul(out=dst, in0=src, scalar1=factor)
+                else:
+                    nc.scalar.activation(out=dst, in_=src, func=ACT.Copy, scale=factor)
+            else:
+                f, cb = (m + NG) // T, (m + NG) % T
+                if cb == 0:
+                    gram_grouped[f] = work.tile([P, C, T], BF16, tag="gram", name="gram", align_bytes=64, bufs=2)
+                dst = gram_grouped[f][:, cb * P : (cb + 1) * P, :].rearrange("p (m s) t -> p m s t", s=T)
+                src = y_ps[m][:].rearrange("p (t s m) -> p m s t", t=T, s=T)
+                if on_vector:
+                    nc.vector.tensor_copy(out=dst, in_=src)
+                else:
+                    nc.scalar.copy(out=dst, in_=src)
+
+        def quantise_gram(f):
+            nc.vector.quantize_mx(
+                out=gram_words[:, f, :].bitcast(FP8X4),
+                scales=gram_scales[:, f, :],
+                in_=gram_grouped[f][:].rearrange("p c t -> p (c t)"),
+            )
+
+        def store(q, j0, j1):
+            nc.sync.dma_start(out=out_v[:, q // 2, 2 * (q % 2) + j0 : 2 * (q % 2) + j1, :], in_=o_sb[q][:, j0:j1, :])
+
+        def pair(q):
+            return 0 <= q < NQ
+
+        flip_patterns(0)
+        flip_x(0)
+        unload_x(0, False)
+        flip_patterns(1)
+        products(LENT + 2)
+
+        for u in range(LAG - NG // 2, NQ + LAG):
+            first, second = 2 * (u - LAG), 2 * (u - LAG) + 1
+            refill = first >= LENT - NG
+            help_step = LAG <= u < NQ and u % HELP == 3
+            draining = u >= NQ
+            group_done = u % 2 == 0 and pair(u - 3)
+
+            if help_step:
+                leave(first, True)
+                products(1)
+            if pair(u):
+                negated_max(2 * u)
+            if pair(u - 2):
+                unload_pair(u - 2)
+            if draining and group_done:
+                quantise_group((u - 4) // 2)
+            if draining and pair(u - 2):
+                regroup_pair(u - 2)
+            if u % 2 == 0 and 0 <= u // 2 < F:
+                quantise_gram(u // 2)
+            if pair(u - 1):
+                exponentials(2 * u - 2)
+            if -1 <= u < NQ - 1:
+                logits(2 * u + 2)
+            if u == NQ:
+                products(2)
+                exponentials(2 * u - 1)
+                flip_pair(u - 1)
+            if not help_step:
+                leave(first, False)
+                if refill:
+                    products(1)
+
+            if pair(u):
+                negated_max(2 * u + 1)
+            if not draining and group_done:
+                quantise_group((u - 4) // 2)
+            if not draining and pair(u - 2):
+                regroup_pair(u - 2)
+            if u % 4 == 1 and 0 < (u + 3) // 4 < NB // 2:
+                unload_x((u + 3) // 4, True)
+            if pair(u - 1) and u < NQ:
+                exponentials(2 * u - 1)
+                flip_pair(u - 1)
+            if -1 <= u < NQ - 1:
+                logits(2 * u + 3)
+            leave(second, u < 1 or u >= NQ + 3)
+            if second == NT - 1:
+                store(second // 2, 0, 1)
+                store(second // 2, 1, 2)
+            elif second > 0:
+                store(second // 2, 0, 2)
+            if refill:
+                products(1)
+            if u % 4 == 0 and 0 < (u + 4) // 4 < NB // 2:
+                flip_x((u + 4) // 4)

@@ -20,7 +20,7 @@ NB = B // P
 NT = NB * F
 NQ = NT // 2
 NG = F * T
-LAG = 6
+LAG = 5
 HELP = 8
 WARM = 5
 LENT = 4
@@ -54,6 +54,8 @@ def tile_hopfieldlayer_pa_t_kernel(tc, x, patterns, out):
 
         ident = keep.tile([P, P], BF16)
         make_identity(nc, ident[:])
+        ident_words = keep.tile([P, P], F32)
+        make_identity(nc, ident_words[:])
         one_column = keep.tile([P, 1], F32)
         unused = keep.tile([P, 1], F32)
         nc.vector.memset(one_column[:], 0.0)
@@ -75,7 +77,7 @@ def tile_hopfieldlayer_pa_t_kernel(tc, x, patterns, out):
                 nc.tensor.transpose(out=bank[:, r, :], in_=blocks(r), identity=ident[:])
             return bank
 
-        xt_ps, s_ps, neg_max, sums, e_sb, et_ps, et_sb, grouped = {}, {}, {}, {}, {}, {}, {}, {}
+        xt_ps, s_ps, neg_max, sums, e_sb, et_ps, grouped = {}, {}, {}, {}, {}, {}, {}
         words, scales, inv_sums, y_ps, o_sb, gram_grouped = {}, {}, {}, {}, {}, {}
 
         def flip_x(h):
@@ -105,12 +107,12 @@ def tile_hopfieldlayer_pa_t_kernel(tc, x, patterns, out):
         def exponentials(m):
             q, j = m // 2, m % 2
             if j == 0:
-                e_sb[q] = work.tile([P, 2 * T, P], BF16, tag="e", name="e")
+                e_sb[q] = work.tile([P, 2, C], BF16, tag="e", name="e")
             if m % F == 0:
                 sums[m // F] = small.tile([P, F], F32, tag="sums", name="sums")
             nc.scalar.activation(
-                out=e_sb[q][:, j * T : (j + 1) * T, :].rearrange("b t p -> b (t p)"),
-                in_=s_ps[m][:],
+                out=e_sb[q][:, j, :].rearrange("b (w p h) -> b w p h", w=2, h=2),
+                in_=s_ps[m][:].rearrange("b (w h p) -> b w p h", w=2, h=2),
                 func=ACT.Exp,
                 bias=neg_max[q][:, j : j + 1],
                 scale=1.0,
@@ -118,29 +120,21 @@ def tile_hopfieldlayer_pa_t_kernel(tc, x, patterns, out):
             )
 
         def flip_pair(q):
-            et_ps[q] = flip(lambda r: e_sb[q][:, r, :])
+            et_ps[q] = flip_banks.tile([P, 2, 2, P], F32, tag="bank", name="flipped_words")
+            for j in range(2):
+                e_words = e_sb[q][:, j, :].bitcast(F32)
+                for w in range(2):
+                    nc.tensor.transpose(
+                        out=et_ps[q][:, j, w, :], in_=e_words[:, w * P : (w + 1) * P], identity=ident_words[:]
+                    )
 
         def unload_pair(q):
-            if q < NQ - 1:
-                et_sb[q] = work.tile([P, 2 * T, P], BF16, tag="et", name="et", bufs=2)
-                nc.vector.tensor_copy(out=et_sb[q][:], in_=et_ps[q][:])
-
-        def regroup_pair(q):
             i, f0 = q // 2, 2 * (q % 2)
             if f0 == 0:
-                grouped[i] = work.tile([P, F, P, T], BF16, tag="grouped", name="grouped", align_bytes=64, bufs=1)
-            dst = grouped[i][:, f0 : f0 + 2]
-            if q < NQ - 1:
-                nc.gpsimd.tensor_scalar(
-                    out=dst,
-                    in0=et_sb[q][:].rearrange("p (j t) b -> p j b t", t=T),
-                    scalar1=1.0,
-                    scalar2=0.0,
-                    op0=ALU.mult,
-                    op1=ALU.add,
-                )
-            else:
-                nc.vector.tensor_copy(out=dst, in_=et_ps[q][:].rearrange("p (j t) b -> p j b t", t=T))
+                grouped[i] = work.tile([P, F, P, T], BF16, tag="grouped", name="grouped", align_bytes=64)
+            nc.vector.tensor_copy(
+                out=grouped[i][:, f0 : f0 + 2].bitcast(F32), in_=et_ps[q][:].rearrange("p j w b -> p j b w")
+            )
 
         def quantise_group(i):
             words[i] = work.tile([P, F * P], U32, tag="words", name="words", align_bytes=64)
@@ -234,7 +228,7 @@ def tile_hopfieldlayer_pa_t_kernel(tc, x, patterns, out):
             refill = first >= LENT - NG
             help_step = LAG <= u < NQ and u % HELP == 3
             draining = u >= NQ
-            group_done = u % 2 == 0 and pair(u - 3)
+            group_done = u % 2 == 1 and pair(u - 2)
 
             if help_step:
                 leave(first, True)
@@ -244,11 +238,9 @@ def tile_hopfieldlayer_pa_t_kernel(tc, x, patterns, out):
             if pair(u - 2):
                 unload_pair(u - 2)
             if draining and group_done:
-                quantise_group((u - 4) // 2)
-            if draining and pair(u - 2):
-                regroup_pair(u - 2)
-            if u % 2 == 0 and 0 <= u // 2 < F:
-                quantise_gram(u // 2)
+                quantise_group((u - 3) // 2)
+            if u % 2 == 1 and 0 <= (u + 1) // 2 < F:
+                quantise_gram((u + 1) // 2)
             if pair(u - 1):
                 exponentials(2 * u - 2)
             if -1 <= u < NQ - 1:
@@ -265,9 +257,7 @@ def tile_hopfieldlayer_pa_t_kernel(tc, x, patterns, out):
             if pair(u):
                 negated_max(2 * u + 1)
             if not draining and group_done:
-                quantise_group((u - 4) // 2)
-            if not draining and pair(u - 2):
-                regroup_pair(u - 2)
+                quantise_group((u - 3) // 2)
             if u % 4 == 1 and 0 < (u + 3) // 4 < NB // 2:
                 unload_x((u + 3) // 4, True)
             if pair(u - 1) and u < NQ:
@@ -275,7 +265,7 @@ def tile_hopfieldlayer_pa_t_kernel(tc, x, patterns, out):
                 flip_pair(u - 1)
             if -1 <= u < NQ - 1:
                 logits(2 * u + 3)
-            leave(second, u < 1 or u >= NQ + 3)
+            leave(second, u < 1 or u >= NQ + 2)
             if second == NT - 1:
                 store(second // 2, 0, 1)
                 store(second // 2, 1, 2)

@@ -20,10 +20,13 @@ NB = B // P
 NT = NB * F
 NQ = NT // 2
 NG = F * T
-LAG = 5
-HELP = 8
-WARM = 5
-LENT = 4
+LAG = 4
+R = 4
+END = 11
+EX = (14, 18, 22, 26, 29, 30)
+HELP = 4
+WARM = 4
+LENT = 2
 FLOPS = 2 * (B * F * C * N + F * C * C * N + B * F * C * C)
 
 
@@ -33,9 +36,9 @@ def tile_hopfieldlayer_pa_t_kernel(tc, x, patterns, out):
         ctx.enter_context(tc.manual_schedule())
         keep = ctx.enter_context(tc.tile_pool(name="keep", bufs=1))
         work = ctx.enter_context(tc.tile_pool(name="work", bufs=3))
-        small = ctx.enter_context(tc.tile_pool(name="small", bufs=6))
-        results = ctx.enter_context(tc.tile_pool(name="results", bufs=4))
-        logit_banks = ctx.enter_context(tc.psum_pool(name="logit_banks", bufs=LENT))
+        small = ctx.enter_context(tc.tile_pool(name="small", bufs=8))
+        results = ctx.enter_context(tc.tile_pool(name="results", bufs=8))
+        logit_banks = ctx.enter_context(tc.psum_pool(name="logit_banks", bufs=4))
         flip_banks = ctx.enter_context(tc.psum_pool(name="flip_banks", bufs=2))
         product_banks = ctx.enter_context(tc.psum_pool(name="product_banks", bufs=2))
 
@@ -45,8 +48,9 @@ def tile_hopfieldlayer_pa_t_kernel(tc, x, patterns, out):
 
         p_sb = keep.tile([P, F, T, N], BF16)
         x_sb = keep.tile([P, NB, F * N], BF16)
-        nc.sync.dma_start(out=p_sb[:, 0:2], in_=p_v[:, 0:2])
+        nc.sync.dma_start(out=p_sb[:, 0:1], in_=p_v[:, 0:1])
         nc.sync.dma_start(out=x_sb[:, 0:2, :], in_=x_v[:, 0:2, :])
+        nc.sync.dma_start(out=p_sb[:, 1:2], in_=p_v[:, 1:2])
         nc.sync.dma_start(out=p_sb[:, 2:4], in_=p_v[:, 2:4])
         nc.sync.dma_start(out=x_sb[:, 2:4, :], in_=x_v[:, 2:4, :])
         for i0 in (4, 8, 12):
@@ -71,9 +75,9 @@ def tile_hopfieldlayer_pa_t_kernel(tc, x, patterns, out):
         gram_words = keep.tile([P, F, C], U32, align_bytes=64)
         gram_scales = keep.tile([P, F, C], U8, align_bytes=64)
 
-        def flip(blocks):
-            bank = flip_banks.tile([P, 2 * T, P], BF16, tag="bank", name="flipped")
-            for r in range(2 * T):
+        def flip(n, blocks):
+            bank = flip_banks.tile([P, n, P], BF16, tag="bank", name="flipped")
+            for r in range(n):
                 nc.tensor.transpose(out=bank[:, r, :], in_=blocks(r), identity=ident[:])
             return bank
 
@@ -81,18 +85,14 @@ def tile_hopfieldlayer_pa_t_kernel(tc, x, patterns, out):
         words, scales, inv_sums, y_ps, o_sb, gram_grouped = {}, {}, {}, {}, {}, {}
 
         def flip_x(h):
-            xt_ps[h] = flip(lambda r: x_sb[:, 2 * h + r // F, (r % F) * N : (r % F + 1) * N])
+            xt_ps[h] = flip(2 * F, lambda r: x_sb[:, 2 * h + r // F, (r % F) * N : (r % F + 1) * N])
 
-        def unload_x(h, on_vector):
-            dst = xt[:, 2 * h : 2 * h + 2].rearrange("n i f p -> n (i f) p")
-            if on_vector:
-                nc.vector.tensor_copy(out=dst, in_=xt_ps[h][:])
-            else:
-                nc.scalar.copy(out=dst, in_=xt_ps[h][:])
+        def unload_x(h):
+            nc.vector.tensor_copy(out=xt[:, 2 * h : 2 * h + 2].rearrange("n i f p -> n (i f) p"), in_=xt_ps[h][:])
 
-        def flip_patterns(h):
-            bank = flip(lambda r: p_sb[:, 2 * h + r // T, r % T, :])
-            nc.vector.tensor_copy(out=pt[:, 2 * h : 2 * h + 2, :].rearrange("n f (t p) -> n (f t) p", p=P), in_=bank[:])
+        def flip_patterns(f0, f1):
+            bank = flip(T * (f1 - f0), lambda r: p_sb[:, f0 + r // T, r % T, :])
+            nc.vector.tensor_copy(out=pt[:, f0:f1, :].rearrange("n f (t p) -> n (f t) p", p=P), in_=bank[:])
 
         def logits(m):
             s_ps[m] = logit_banks.tile([P, C], F32, tag="bank", name="s")
@@ -108,15 +108,14 @@ def tile_hopfieldlayer_pa_t_kernel(tc, x, patterns, out):
             q, j = m // 2, m % 2
             if j == 0:
                 e_sb[q] = work.tile([P, 2, C], BF16, tag="e", name="e")
-            if m % F == 0:
-                sums[m // F] = small.tile([P, F], F32, tag="sums", name="sums")
+                sums[q] = small.tile([P, 2], F32, tag="sums", name="sums")
             nc.scalar.activation(
                 out=e_sb[q][:, j, :].rearrange("b (w p h) -> b w p h", w=2, h=2),
                 in_=s_ps[m][:].rearrange("b (w h p) -> b w p h", w=2, h=2),
                 func=ACT.Exp,
                 bias=neg_max[q][:, j : j + 1],
                 scale=1.0,
-                accum_out=sums[m // F][:, m % F : m % F + 1],
+                accum_out=sums[q][:, j : j + 1],
             )
 
         def flip_pair(q):
@@ -129,35 +128,31 @@ def tile_hopfieldlayer_pa_t_kernel(tc, x, patterns, out):
                     )
 
         def unload_pair(q):
-            i, f0 = q // 2, 2 * (q % 2)
-            if f0 == 0:
-                grouped[i] = work.tile([P, F, P, T], BF16, tag="grouped", name="grouped", align_bytes=64)
-            nc.vector.tensor_copy(
-                out=grouped[i][:, f0 : f0 + 2].bitcast(F32), in_=et_ps[q][:].rearrange("p j w b -> p j b w")
-            )
+            grouped[q] = work.tile([P, 2, P, T], BF16, tag="grouped", name="grouped", align_bytes=64)
+            nc.vector.tensor_copy(out=grouped[q][:].bitcast(F32), in_=et_ps[q][:].rearrange("p j w b -> p j b w"))
 
-        def quantise_group(i):
-            words[i] = work.tile([P, F * P], U32, tag="words", name="words", align_bytes=64)
-            scales[i] = work.tile([P, F * P], U8, tag="scales", name="scales", align_bytes=64)
+        def quantise_pair(q):
+            words[q] = work.tile([P, 2 * P], U32, tag="words", name="words", align_bytes=64, bufs=6)
+            scales[q] = work.tile([P, 2 * P], U8, tag="scales", name="scales", align_bytes=64, bufs=6)
             nc.vector.quantize_mx(
-                out=words[i][:].bitcast(FP8X4),
-                scales=scales[i][:],
-                in_=grouped[i][:].rearrange("p f b t -> p (f b t)"),
+                out=words[q][:].bitcast(FP8X4),
+                scales=scales[q][:],
+                in_=grouped[q][:].rearrange("p j b t -> p (j b t)"),
             )
-            inv_sums[i] = small.tile([P, F], F32, tag="inv_sums", name="inv_sums")
-            nc.vector.reciprocal(out=inv_sums[i][:], in_=sums[i][:])
+            inv_sums[q] = small.tile([P, 2], F32, tag="inv_sums", name="inv_sums")
+            nc.vector.reciprocal(out=inv_sums[q][:], in_=sums[q][:])
 
-        def product(m):
-            if m < LENT - NG or m >= NT - 2 * LAG + 2:
+        def product(m, lent):
+            if lent:
                 y_ps[m] = logit_banks.tile([P, C], F32, tag="bank", name="y")
             else:
                 y_ps[m] = product_banks.tile([P, C], F32, tag="bank", name="y")
             if m >= 0:
-                i, f = m // F, m % F
+                q, j, f = m // 2, m % 2, m % F
                 nc.tensor.matmul_mx(
                     out=y_ps[m][:],
-                    lhsT=words[i][:, f * P : (f + 1) * P].bitcast(FP8X4),
-                    lhsT_scale=scales[i][:, f * P : (f + 1) * P],
+                    lhsT=words[q][:, j * P : (j + 1) * P].bitcast(FP8X4),
+                    lhsT_scale=scales[q][:, j * P : (j + 1) * P],
                     rhs=gram_words[:, f, :].bitcast(FP8X4),
                     rhs_scale=gram_scales[:, f, :],
                     start=True,
@@ -177,18 +172,17 @@ def tile_hopfieldlayer_pa_t_kernel(tc, x, patterns, out):
 
         issued = [-NG]
 
-        def products(n):
+        def products(n, lent=False):
             for r in range(n):
-                if issued[0] < NT:
-                    product(issued[0])
-                    issued[0] += 1
+                product(issued[0], lent)
+                issued[0] += 1
 
         def leave(m, on_vector):
             if m >= 0:
                 q, j = m // 2, m % 2
                 if j == 0:
                     o_sb[q] = results.tile([P, 2, C], F32, tag="o", name="o")
-                dst, src, factor = o_sb[q][:, j, :], y_ps[m][:], inv_sums[m // F][:, m % F : m % F + 1]
+                dst, src, factor = o_sb[q][:, j, :], y_ps[m][:], inv_sums[q][:, j : j + 1]
                 if on_vector:
                     nc.vector.tensor_scalar_mul(out=dst, in0=src, scalar1=factor)
                 else:
@@ -214,64 +208,112 @@ def tile_hopfieldlayer_pa_t_kernel(tc, x, patterns, out):
         def store(q, j0, j1):
             nc.sync.dma_start(out=out_v[:, q // 2, 2 * (q % 2) + j0 : 2 * (q % 2) + j1, :], in_=o_sb[q][:, j0:j1, :])
 
-        def pair(q):
-            return 0 <= q < NQ
+        left = [-NG]
 
-        flip_patterns(0)
+        def leave_next(on_vector):
+            m = left[0]
+            left[0] += 1
+            leave(m, on_vector)
+            if m >= NT - 2:
+                store(m // 2, m % 2, m % 2 + 1)
+            elif m > 0 and m % 2 == 1:
+                store(m // 2, 0, 2)
+            if LENT - NG <= m and not in_tail:
+                products(1)
+
+        flip_patterns(0, 1)
         flip_x(0)
-        unload_x(0, False)
-        flip_patterns(1)
-        products(LENT + 2)
+        unload_x(0)
+        products(LENT, True)
+        flip_patterns(1, 2)
+        logits(0)
+        products(1)
+        logits(1)
+        products(1)
+        leave_next(False)
+        leave_next(False)
+        gram_done = 0
+        in_tail = []
 
-        for u in range(LAG - NG // 2, NQ + LAG):
-            first, second = 2 * (u - LAG), 2 * (u - LAG) + 1
-            refill = first >= LENT - NG
-            help_step = LAG <= u < NQ and u % HELP == 3
-            draining = u >= NQ
-            group_done = u % 2 == 1 and pair(u - 2)
-
-            if help_step:
-                leave(first, True)
-                products(1)
-            if pair(u):
-                negated_max(2 * u)
-            if pair(u - 2):
+        for u in range(NQ - 1):
+            ready = max(0, 2 * u - R)
+            if u in EX and left[0] < ready:
+                leave_next(True)
+            negated_max(2 * u)
+            if u == 0:
+                flip_patterns(2, 4)
+            if u >= 2:
                 unload_pair(u - 2)
-            if draining and group_done:
-                quantise_group((u - 3) // 2)
-            if u % 2 == 1 and 0 <= (u + 1) // 2 < F:
-                quantise_gram((u + 1) // 2)
-            if pair(u - 1):
+            if gram_done < F and left[0] >= (gram_done + 1) * T - NG:
+                quantise_gram(gram_done)
+                gram_done += 1
+            if u >= 1:
                 exponentials(2 * u - 2)
-            if -1 <= u < NQ - 1:
-                logits(2 * u + 2)
-            if u == NQ:
-                products(2)
-                exponentials(2 * u - 1)
-                flip_pair(u - 1)
-            if not help_step:
-                leave(first, False)
-                if refill:
-                    products(1)
+            logits(2 * u + 2)
+            if left[0] < ready:
+                leave_next(False)
 
-            if pair(u):
-                negated_max(2 * u + 1)
-            if not draining and group_done:
-                quantise_group((u - 3) // 2)
+            negated_max(2 * u + 1)
+            if u >= 2:
+                quantise_pair(u - 2)
             if u % 4 == 1 and 0 < (u + 3) // 4 < NB // 2:
-                unload_x((u + 3) // 4, True)
-            if pair(u - 1) and u < NQ:
+                unload_x((u + 3) // 4)
+            if u >= 1:
                 exponentials(2 * u - 1)
                 flip_pair(u - 1)
-            if -1 <= u < NQ - 1:
-                logits(2 * u + 3)
-            leave(second, u < 1 or u >= NQ + 2)
-            if second == NT - 1:
-                store(second // 2, 0, 1)
-                store(second // 2, 1, 2)
-            elif second > 0:
-                store(second // 2, 0, 2)
-            if refill:
-                products(1)
+            logits(2 * u + 3)
+            if left[0] < ready:
+                leave_next(False)
             if u % 4 == 0 and 0 < (u + 4) // 4 < NB // 2:
                 flip_x((u + 4) // 4)
+
+        in_tail.append(1)
+        lent = []
+        quantised = [2 * (NQ - 3)]
+        def more():
+            while issued[0] < quantised[0] and (lent or len(normal) < 2 or normal[-2] < left[0]):
+                if len(normal) >= 2 and normal[-2] < left[0]:
+                    normal.append(issued[0])
+                    products(1)
+                else:
+                    products(1, lent.pop())
+        normal = [issued[0] - 2, issued[0] - 1]
+        def lv(v):
+            if left[0] < issued[0]:
+                leave_next(v)
+            more()
+        negated_max(NT - 2)
+        exponentials(NT - 4)
+        lent.append(True)
+        lv(False)
+        negated_max(NT - 1)
+        exponentials(NT - 3)
+        lent.append(True)
+        flip_pair(NQ - 2)
+        unload_pair(NQ - 3)
+        more()
+        exponentials(NT - 2)
+        lent.append(True)
+        lv(True)
+        quantise_pair(NQ - 3)
+        quantised[0] += 2
+        exponentials(NT - 1)
+        lent.append(True)
+        flip_pair(NQ - 1)
+        more()
+        lv(False)
+        unload_pair(NQ - 2)
+        lv(True)
+        quantise_pair(NQ - 2)
+        quantised[0] += 2
+        more()
+        lv(False)
+        unload_pair(NQ - 1)
+        lv(False)
+        quantise_pair(NQ - 1)
+        quantised[0] += 2
+        more()
+        v = True
+        while left[0] < NT:
+            lv(v)
+            v = not v

@@ -21,9 +21,11 @@ NT = NB * F
 NQ = NT // 2
 NG = F * T
 LAG = 4
-R = 4
+R = 6
+ONE = 8
+SINGLE = 4
 END = 11
-EX = (14, 18, 22, 26, 29, 30)
+HELP_FROM = 18
 HELP = 4
 WARM = 4
 LENT = 2
@@ -108,14 +110,27 @@ def tile_hopfieldlayer_pa_t_kernel(tc, x, patterns, out):
             q, j = m // 2, m % 2
             if j == 0:
                 e_sb[q] = work.tile([P, 2, C], BF16, tag="e", name="e")
-                sums[q] = small.tile([P, 2], F32, tag="sums", name="sums")
+            if m % F == 0:
+                sums[m // F] = small.tile([P, F], F32, tag="sums", name="sums")
             nc.scalar.activation(
                 out=e_sb[q][:, j, :].rearrange("b (w p h) -> b w p h", w=2, h=2),
                 in_=s_ps[m][:].rearrange("b (w h p) -> b w p h", w=2, h=2),
                 func=ACT.Exp,
                 bias=neg_max[q][:, j : j + 1],
                 scale=1.0,
-                accum_out=sums[q][:, j : j + 1],
+                accum_out=sums[m // F][:, m % F : m % F + 1],
+            )
+
+        def flip_tile(m):
+            q, j = m // 2, m % 2
+            et_ps[m, 0] = flip_banks.tile([P, 2, P], F32, tag="bank", name="flipped_tile")
+            e_words = e_sb[q][:, j, :].bitcast(F32)
+            for w in range(2):
+                nc.tensor.transpose(out=et_ps[m, 0][:, w, :], in_=e_words[:, w * P : (w + 1) * P], identity=ident_words[:])
+
+        def unload_tile(m):
+            nc.vector.tensor_copy(
+                out=grouped[m // F][:, m % F].bitcast(F32), in_=et_ps[m, 0][:].rearrange("p w b -> p b w")
             )
 
         def flip_pair(q):
@@ -128,19 +143,30 @@ def tile_hopfieldlayer_pa_t_kernel(tc, x, patterns, out):
                     )
 
         def unload_pair(q):
-            grouped[q] = work.tile([P, 2, P, T], BF16, tag="grouped", name="grouped", align_bytes=64)
-            nc.vector.tensor_copy(out=grouped[q][:].bitcast(F32), in_=et_ps[q][:].rearrange("p j w b -> p j b w"))
+            i, f0 = q // 2, 2 * (q % 2)
+            if f0 == 0:
+                grouped[i] = work.tile([P, F, P, T], BF16, tag="grouped", name="grouped", align_bytes=64)
+            nc.vector.tensor_copy(
+                out=grouped[i][:, f0 : f0 + 2].bitcast(F32), in_=et_ps[q][:].rearrange("p j w b -> p j b w")
+            )
+
+        def quantise(i, f0, f1):
+            if f0 == 0:
+                words[i] = work.tile([P, F * P], U32, tag="words", name="words", align_bytes=64, bufs=4)
+                scales[i] = work.tile([P, F * P], U8, tag="scales", name="scales", align_bytes=64, bufs=4)
+                inv_sums[i] = small.tile([P, F], F32, tag="inv_sums", name="inv_sums")
+            nc.vector.quantize_mx(
+                out=words[i][:, f0 * P : f1 * P].bitcast(FP8X4),
+                scales=scales[i][:, f0 * P : f1 * P],
+                in_=grouped[i][:, f0:f1].rearrange("p f b t -> p (f b t)"),
+            )
+            nc.vector.reciprocal(out=inv_sums[i][:, f0:f1], in_=sums[i][:, f0:f1])
 
         def quantise_pair(q):
-            words[q] = work.tile([P, 2 * P], U32, tag="words", name="words", align_bytes=64, bufs=6)
-            scales[q] = work.tile([P, 2 * P], U8, tag="scales", name="scales", align_bytes=64, bufs=6)
-            nc.vector.quantize_mx(
-                out=words[q][:].bitcast(FP8X4),
-                scales=scales[q][:],
-                in_=grouped[q][:].rearrange("p j b t -> p (j b t)"),
-            )
-            inv_sums[q] = small.tile([P, 2], F32, tag="inv_sums", name="inv_sums")
-            nc.vector.reciprocal(out=inv_sums[q][:], in_=sums[q][:])
+            if q >= NQ - SINGLE:
+                quantise(q // 2, 2 * (q % 2), 2 * (q % 2) + 2)
+            elif q % 2 == 1:
+                quantise(q // 2, 0, F)
 
         def product(m, lent):
             if lent:
@@ -148,11 +174,11 @@ def tile_hopfieldlayer_pa_t_kernel(tc, x, patterns, out):
             else:
                 y_ps[m] = product_banks.tile([P, C], F32, tag="bank", name="y")
             if m >= 0:
-                q, j, f = m // 2, m % 2, m % F
+                i, f = m // F, m % F
                 nc.tensor.matmul_mx(
                     out=y_ps[m][:],
-                    lhsT=words[q][:, j * P : (j + 1) * P].bitcast(FP8X4),
-                    lhsT_scale=scales[q][:, j * P : (j + 1) * P],
+                    lhsT=words[i][:, f * P : (f + 1) * P].bitcast(FP8X4),
+                    lhsT_scale=scales[i][:, f * P : (f + 1) * P],
                     rhs=gram_words[:, f, :].bitcast(FP8X4),
                     rhs_scale=gram_scales[:, f, :],
                     start=True,
@@ -182,7 +208,7 @@ def tile_hopfieldlayer_pa_t_kernel(tc, x, patterns, out):
                 q, j = m // 2, m % 2
                 if j == 0:
                     o_sb[q] = results.tile([P, 2, C], F32, tag="o", name="o")
-                dst, src, factor = o_sb[q][:, j, :], y_ps[m][:], inv_sums[q][:, j : j + 1]
+                dst, src, factor = o_sb[q][:, j, :], y_ps[m][:], inv_sums[m // F][:, m % F : m % F + 1]
                 if on_vector:
                     nc.vector.tensor_scalar_mul(out=dst, in0=src, scalar1=factor)
                 else:
@@ -209,12 +235,13 @@ def tile_hopfieldlayer_pa_t_kernel(tc, x, patterns, out):
             nc.sync.dma_start(out=out_v[:, q // 2, 2 * (q % 2) + j0 : 2 * (q % 2) + j1, :], in_=o_sb[q][:, j0:j1, :])
 
         left = [-NG]
+        in_tail = []
 
         def leave_next(on_vector):
             m = left[0]
             left[0] += 1
             leave(m, on_vector)
-            if m >= NT - 2:
+            if m >= NT - ONE:
                 store(m // 2, m % 2, m % 2 + 1)
             elif m > 0 and m % 2 == 1:
                 store(m // 2, 0, 2)
@@ -232,23 +259,28 @@ def tile_hopfieldlayer_pa_t_kernel(tc, x, patterns, out):
         products(1)
         leave_next(False)
         leave_next(False)
-        gram_done = 0
-        in_tail = []
+        negated_max(0)
+        negated_max(1)
+        flip_patterns(2, 4)
+        leave_next(False)
+        leave_next(False)
+        logits(2)
+        logits(3)
+        quantise_gram(0)
+        flip_x(1)
+        gram_done = 1
 
-        for u in range(NQ - 1):
+        for u in range(1, NQ - 1):
             ready = max(0, 2 * u - R)
-            if u in EX and left[0] < ready:
+            if u >= HELP_FROM and u % HELP == 2 and left[0] < ready:
                 leave_next(True)
             negated_max(2 * u)
-            if u == 0:
-                flip_patterns(2, 4)
             if u >= 2:
                 unload_pair(u - 2)
             if gram_done < F and left[0] >= (gram_done + 1) * T - NG:
                 quantise_gram(gram_done)
                 gram_done += 1
-            if u >= 1:
-                exponentials(2 * u - 2)
+            exponentials(2 * u - 2)
             logits(2 * u + 2)
             if left[0] < ready:
                 leave_next(False)
@@ -258,9 +290,8 @@ def tile_hopfieldlayer_pa_t_kernel(tc, x, patterns, out):
                 quantise_pair(u - 2)
             if u % 4 == 1 and 0 < (u + 3) // 4 < NB // 2:
                 unload_x((u + 3) // 4)
-            if u >= 1:
-                exponentials(2 * u - 1)
-                flip_pair(u - 1)
+            exponentials(2 * u - 1)
+            flip_pair(u - 1)
             logits(2 * u + 3)
             if left[0] < ready:
                 leave_next(False)
@@ -270,49 +301,54 @@ def tile_hopfieldlayer_pa_t_kernel(tc, x, patterns, out):
         in_tail.append(1)
         lent = []
         quantised = [2 * (NQ - 3)]
+        normal = [issued[0] - 2, issued[0] - 1]
         def more():
-            while issued[0] < quantised[0] and (lent or len(normal) < 2 or normal[-2] < left[0]):
-                if len(normal) >= 2 and normal[-2] < left[0]:
+            while issued[0] < quantised[0] and (lent or normal[-2] < left[0]):
+                if lent:
+                    products(1, lent.pop())
+                else:
                     normal.append(issued[0])
                     products(1)
-                else:
-                    products(1, lent.pop())
-        normal = [issued[0] - 2, issued[0] - 1]
+        def E(m):
+            exponentials(m)
+            lent.append(True)
+            more()
         def lv(v):
             if left[0] < issued[0]:
                 leave_next(v)
             more()
+        def Q(q):
+            quantise_pair(q)
+            quantised[0] += 2
+            more()
+        def QT(m):
+            quantise(m // F, m % F, m % F + 1)
+            quantised[0] += 1
+            more()
         negated_max(NT - 2)
-        exponentials(NT - 4)
-        lent.append(True)
+        E(NT - 4)
         lv(False)
         negated_max(NT - 1)
-        exponentials(NT - 3)
-        lent.append(True)
+        E(NT - 3)
         flip_pair(NQ - 2)
+        lv(False)
         unload_pair(NQ - 3)
-        more()
-        exponentials(NT - 2)
-        lent.append(True)
+        E(NT - 2)
         lv(True)
-        quantise_pair(NQ - 3)
-        quantised[0] += 2
-        exponentials(NT - 1)
-        lent.append(True)
-        flip_pair(NQ - 1)
-        more()
+        Q(NQ - 3)
+        flip_tile(NT - 2)
         lv(False)
+        E(NT - 1)
         unload_pair(NQ - 2)
-        lv(True)
-        quantise_pair(NQ - 2)
-        quantised[0] += 2
-        more()
+        flip_tile(NT - 1)
         lv(False)
-        unload_pair(NQ - 1)
+        unload_tile(NT - 2)
+        Q(NQ - 2)
+        QT(NT - 2)
         lv(False)
-        quantise_pair(NQ - 1)
-        quantised[0] += 2
-        more()
+        unload_tile(NT - 1)
+        lv(False)
+        QT(NT - 1)
         v = True
         while left[0] < NT:
             lv(v)

@@ -38,8 +38,8 @@ def tile_hopfieldlayer_pa_t_kernel(tc, x, patterns, out):
         ctx.enter_context(tc.manual_schedule())
         keep = ctx.enter_context(tc.tile_pool(name="keep", bufs=1))
         work = ctx.enter_context(tc.tile_pool(name="work", bufs=3))
-        small = ctx.enter_context(tc.tile_pool(name="small", bufs=8))
-        results = ctx.enter_context(tc.tile_pool(name="results", bufs=8))
+        small = ctx.enter_context(tc.tile_pool(name="small", bufs=32))
+        results = ctx.enter_context(tc.tile_pool(name="results", bufs=32))
         logit_banks = ctx.enter_context(tc.psum_pool(name="logit_banks", bufs=4))
         flip_banks = ctx.enter_context(tc.psum_pool(name="flip_banks", bufs=2))
         product_banks = ctx.enter_context(tc.psum_pool(name="product_banks", bufs=2))
@@ -155,12 +155,12 @@ def tile_hopfieldlayer_pa_t_kernel(tc, x, patterns, out):
                 words[i] = work.tile([P, F * P], U32, tag="words", name="words", align_bytes=64, bufs=4)
                 scales[i] = work.tile([P, F * P], U8, tag="scales", name="scales", align_bytes=64, bufs=4)
                 inv_sums[i] = small.tile([P, F], F32, tag="inv_sums", name="inv_sums")
+            nc.vector.reciprocal(out=inv_sums[i][:, f0:f1], in_=sums[i][:, f0:f1])
             nc.vector.quantize_mx(
                 out=words[i][:, f0 * P : f1 * P].bitcast(FP8X4),
                 scales=scales[i][:, f0 * P : f1 * P],
                 in_=grouped[i][:, f0:f1].rearrange("p f b t -> p (f b t)"),
             )
-            nc.vector.reciprocal(out=inv_sums[i][:, f0:f1], in_=sums[i][:, f0:f1])
 
         def quantise_pair(q):
             if q >= NQ - SINGLE:

@@ -25,7 +25,7 @@ R = 6
 ONE = 8
 SINGLE = 4
 END = 11
-HELP_FROM = 18
+HELP_FROM = 14
 HELP = 4
 WARM = 4
 LENT = 2
@@ -51,8 +51,9 @@ def tile_hopfieldlayer_pa_t_kernel(tc, x, patterns, out):
         p_sb = keep.tile([P, F, T, N], BF16)
         x_sb = keep.tile([P, NB, F * N], BF16)
         nc.sync.dma_start(out=p_sb[:, 0:1], in_=p_v[:, 0:1])
-        nc.sync.dma_start(out=x_sb[:, 0:2, :], in_=x_v[:, 0:2, :])
+        nc.sync.dma_start(out=x_sb[:, 0:1, :], in_=x_v[:, 0:1, :])
         nc.sync.dma_start(out=p_sb[:, 1:2], in_=p_v[:, 1:2])
+        nc.sync.dma_start(out=x_sb[:, 1:2, :], in_=x_v[:, 1:2, :])
         nc.sync.dma_start(out=p_sb[:, 2:4], in_=p_v[:, 2:4])
         nc.sync.dma_start(out=x_sb[:, 2:4, :], in_=x_v[:, 2:4, :])
         for i0 in (4, 8, 12):
@@ -77,8 +78,8 @@ def tile_hopfieldlayer_pa_t_kernel(tc, x, patterns, out):
         gram_words = keep.tile([P, F, C], U32, align_bytes=64)
         gram_scales = keep.tile([P, F, C], U8, align_bytes=64)
 
-        def flip(n, blocks):
-            bank = flip_banks.tile([P, n, P], BF16, tag="bank", name="flipped")
+        def flip(n, blocks, pool=flip_banks):
+            bank = pool.tile([P, n, P], BF16, tag="bank", name="flipped")
             for r in range(n):
                 nc.tensor.transpose(out=bank[:, r, :], in_=blocks(r), identity=ident[:])
             return bank
@@ -92,8 +93,15 @@ def tile_hopfieldlayer_pa_t_kernel(tc, x, patterns, out):
         def unload_x(h):
             nc.vector.tensor_copy(out=xt[:, 2 * h : 2 * h + 2].rearrange("n i f p -> n (i f) p"), in_=xt_ps[h][:])
 
-        def flip_patterns(f0, f1):
-            bank = flip(T * (f1 - f0), lambda r: p_sb[:, f0 + r // T, r % T, :])
+        def first_x(i, on_vector):
+            bank = flip(F, lambda r: x_sb[:, i, r * N : (r + 1) * N])
+            if on_vector:
+                nc.vector.tensor_copy(out=xt[:, i], in_=bank[:])
+            else:
+                nc.scalar.copy(out=xt[:, i], in_=bank[:])
+
+        def flip_patterns(f0, f1, pool=flip_banks):
+            bank = flip(T * (f1 - f0), lambda r: p_sb[:, f0 + r // T, r % T, :], pool)
             nc.vector.tensor_copy(out=pt[:, f0:f1, :].rearrange("n f (t p) -> n (f t) p", p=P), in_=bank[:])
 
         def logits(m):
@@ -249,13 +257,13 @@ def tile_hopfieldlayer_pa_t_kernel(tc, x, patterns, out):
                 products(1)
 
         flip_patterns(0, 1)
-        flip_x(0)
-        unload_x(0)
+        first_x(0, False)
+        flip_patterns(1, 2, logit_banks)
         products(LENT, True)
-        flip_patterns(1, 2)
+        first_x(1, True)
         logits(0)
-        products(1)
         logits(1)
+        products(1)
         products(1)
         leave_next(False)
         leave_next(False)
@@ -300,18 +308,28 @@ def tile_hopfieldlayer_pa_t_kernel(tc, x, patterns, out):
 
         in_tail.append(1)
         lent = []
-        quantised = [2 * (NQ - 3)]
         normal = [issued[0] - 2, issued[0] - 1]
+        gone = [0]
+        quantised = [2 * (NQ - 3)]
         def more():
-            while issued[0] < quantised[0] and (lent or normal[-2] < left[0]):
-                if lent:
-                    products(1, lent.pop())
-                else:
+            while issued[0] < quantised[0]:
+                k = len(lent)
+                if (k < gone[0]) if k < 4 else lent[k - 4] < left[0]:
+                    lent.append(issued[0])
+                    products(1, True)
+                elif normal[-2] < left[0]:
                     normal.append(issued[0])
                     products(1)
+                else:
+                    return
         def E(m):
             exponentials(m)
-            lent.append(True)
+            gone[0] += 1
+            more()
+        def X(m):
+            exponentials(m)
+            flip_tile(m)
+            gone[0] += 1
             more()
         def lv(v):
             if left[0] < issued[0]:
@@ -325,6 +343,7 @@ def tile_hopfieldlayer_pa_t_kernel(tc, x, patterns, out):
             quantise(m // F, m % F, m % F + 1)
             quantised[0] += 1
             more()
+
         negated_max(NT - 2)
         E(NT - 4)
         lv(False)
@@ -333,23 +352,23 @@ def tile_hopfieldlayer_pa_t_kernel(tc, x, patterns, out):
         flip_pair(NQ - 2)
         lv(False)
         unload_pair(NQ - 3)
-        E(NT - 2)
+        X(NT - 2)
         lv(True)
         Q(NQ - 3)
-        flip_tile(NT - 2)
         lv(False)
-        E(NT - 1)
+        lv(True)
         unload_pair(NQ - 2)
-        flip_tile(NT - 1)
+        X(NT - 1)
         lv(False)
         unload_tile(NT - 2)
         Q(NQ - 2)
         QT(NT - 2)
         lv(False)
         unload_tile(NT - 1)
-        lv(False)
+        lv(True)
         QT(NT - 1)
-        v = True
+        v = False
         while left[0] < NT:
             lv(v)
             v = not v
+        assert left[0] == NT, left[0]

@@ -22,7 +22,6 @@ NQ = NT // 2
 NG = F * T
 LAG = 4
 R = 6
-ONE = 8
 SINGLE = 4
 END = 11
 HELP_FROM = 14
@@ -249,9 +248,7 @@ def tile_hopfieldlayer_pa_t_kernel(tc, x, patterns, out):
             m = left[0]
             left[0] += 1
             leave(m, on_vector)
-            if m >= NT - ONE:
-                store(m // 2, m % 2, m % 2 + 1)
-            elif m > 0 and m % 2 == 1:
+            if m > 0 and m % 2 == 1:
                 store(m // 2, 0, 2)
             if LENT - NG <= m and not in_tail:
                 products(1)
@@ -365,7 +362,6 @@ def tile_hopfieldlayer_pa_t_kernel(tc, x, patterns, out):
         QT(NT - 2)
         lv(False)
         unload_tile(NT - 1)
-        lv(True)
         QT(NT - 1)
         v = False
         while left[0] < NT:

@@ -43,9 +43,9 @@ def tile_hopfieldlayer_pa_t_kernel(tc, x, patterns, out):
         flip_banks = ctx.enter_context(tc.psum_pool(name="flip_banks", bufs=2))
         product_banks = ctx.enter_context(tc.psum_pool(name="product_banks", bufs=2))
 
-        x_v = x.rearrange("(p i) f n -> p i (f n)", i=NB)
+        x_v = x.rearrange("(i p) f n -> p i (f n)", i=NB)
         p_v = patterns.rearrange("f (p t) n -> p f t n", t=T)
-        out_v = out.rearrange("(p i) f c -> p i f c", i=NB)
+        out_v = out.rearrange("(i p) f c -> p i f c", i=NB)
 
         p_sb = keep.tile([P, F, T, N], BF16)
         x_sb = keep.tile([P, NB, F * N], BF16)

@@ -20,13 +20,11 @@ NB = B // P
 NT = NB * F
 NQ = NT // 2
 NG = F * T
-LAG = 4
-R = 6
-SINGLE = 4
-END = 11
-HELP_FROM = 14
-HELP = 4
+LAST_PAIRS = 4
+FIRST_EXTRA = 13
+EVERY = 4
 WARM = 4
+LOGIT_BANKS = 4
 LENT = 2
 FLOPS = 2 * (B * F * C * N + F * C * C * N + B * F * C * C)
 
@@ -37,9 +35,9 @@ def tile_hopfieldlayer_pa_t_kernel(tc, x, patterns, out):
         ctx.enter_context(tc.manual_schedule())
         keep = ctx.enter_context(tc.tile_pool(name="keep", bufs=1))
         work = ctx.enter_context(tc.tile_pool(name="work", bufs=3))
-        small = ctx.enter_context(tc.tile_pool(name="small", bufs=32))
-        results = ctx.enter_context(tc.tile_pool(name="results", bufs=32))
-        logit_banks = ctx.enter_context(tc.psum_pool(name="logit_banks", bufs=4))
+        small = ctx.enter_context(tc.tile_pool(name="small", bufs=NQ))
+        results = ctx.enter_context(tc.tile_pool(name="results", bufs=NQ))
+        logit_banks = ctx.enter_context(tc.psum_pool(name="logit_banks", bufs=LOGIT_BANKS))
         flip_banks = ctx.enter_context(tc.psum_pool(name="flip_banks", bufs=2))
         product_banks = ctx.enter_context(tc.psum_pool(name="product_banks", bufs=2))
 
@@ -77,7 +75,7 @@ def tile_hopfieldlayer_pa_t_kernel(tc, x, patterns, out):
         gram_words = keep.tile([P, F, C], U32, align_bytes=64)
         gram_scales = keep.tile([P, F, C], U8, align_bytes=64)
 
-        def flip(n, blocks, pool=flip_banks):
+        def flip(n, blocks, pool):
             bank = pool.tile([P, n, P], BF16, tag="bank", name="flipped")
             for r in range(n):
                 nc.tensor.transpose(out=bank[:, r, :], in_=blocks(r), identity=ident[:])
@@ -87,19 +85,19 @@ def tile_hopfieldlayer_pa_t_kernel(tc, x, patterns, out):
         words, scales, inv_sums, y_ps, o_sb, gram_grouped = {}, {}, {}, {}, {}, {}
 
         def flip_x(h):
-            xt_ps[h] = flip(2 * F, lambda r: x_sb[:, 2 * h + r // F, (r % F) * N : (r % F + 1) * N])
+            xt_ps[h] = flip(2 * F, lambda r: x_sb[:, 2 * h + r // F, (r % F) * N : (r % F + 1) * N], flip_banks)
 
         def unload_x(h):
             nc.vector.tensor_copy(out=xt[:, 2 * h : 2 * h + 2].rearrange("n i f p -> n (i f) p"), in_=xt_ps[h][:])
 
-        def first_x(i, on_vector):
-            bank = flip(F, lambda r: x_sb[:, i, r * N : (r + 1) * N])
+        def copy_x(i, pool, on_vector):
+            bank = flip(F, lambda r: x_sb[:, i, r * N : (r + 1) * N], pool)
             if on_vector:
                 nc.vector.tensor_copy(out=xt[:, i], in_=bank[:])
             else:
                 nc.scalar.copy(out=xt[:, i], in_=bank[:])
 
-        def flip_patterns(f0, f1, pool=flip_banks):
+        def flip_patterns(f0, f1, pool):
             bank = flip(T * (f1 - f0), lambda r: p_sb[:, f0 + r // T, r % T, :], pool)
             nc.vector.tensor_copy(out=pt[:, f0:f1, :].rearrange("n f (t p) -> n (f t) p", p=P), in_=bank[:])
 
@@ -170,7 +168,7 @@ def tile_hopfieldlayer_pa_t_kernel(tc, x, patterns, out):
             )
 
         def quantise_pair(q):
-            if q >= NQ - SINGLE:
+            if q >= NQ - LAST_PAIRS:
                 quantise(q // 2, 2 * (q % 2), 2 * (q % 2) + 2)
             elif q % 2 == 1:
                 quantise(q // 2, 0, F)
@@ -238,47 +236,48 @@ def tile_hopfieldlayer_pa_t_kernel(tc, x, patterns, out):
                 in_=gram_grouped[f][:].rearrange("p c t -> p (c t)"),
             )
 
-        def store(q, j0, j1):
-            nc.sync.dma_start(out=out_v[:, q // 2, 2 * (q % 2) + j0 : 2 * (q % 2) + j1, :], in_=o_sb[q][:, j0:j1, :])
+        def store(q):
+            nc.sync.dma_start(out=out_v[:, q // 2, 2 * (q % 2) : 2 * (q % 2) + 2, :], in_=o_sb[q][:])
 
         left = [-NG]
-        in_tail = []
 
         def leave_next(on_vector):
             m = left[0]
             left[0] += 1
             leave(m, on_vector)
             if m > 0 and m % 2 == 1:
-                store(m // 2, 0, 2)
-            if LENT - NG <= m and not in_tail:
+                store(m // 2)
+
+        def leave_and_refill(on_vector):
+            leave_next(on_vector)
+            if left[0] > LENT - NG:
                 products(1)
 
-        flip_patterns(0, 1)
-        first_x(0, False)
+        flip_patterns(0, 1, flip_banks)
+        copy_x(0, flip_banks, on_vector=False)
         flip_patterns(1, 2, logit_banks)
+        copy_x(1, product_banks, on_vector=True)
         products(LENT, True)
-        first_x(1, True)
         logits(0)
         logits(1)
-        products(1)
-        products(1)
-        leave_next(False)
-        leave_next(False)
+        products(2)
+        leave_and_refill(False)
+        leave_and_refill(False)
         negated_max(0)
         negated_max(1)
-        flip_patterns(2, 4)
-        leave_next(False)
-        leave_next(False)
+        flip_patterns(2, 4, flip_banks)
+        leave_and_refill(False)
+        leave_and_refill(False)
         logits(2)
         logits(3)
         quantise_gram(0)
         flip_x(1)
         gram_done = 1
 
+        def extra(u):
+            return u >= FIRST_EXTRA and (u - FIRST_EXTRA) % EVERY == 0
+
         for u in range(1, NQ - 1):
-            ready = max(0, 2 * u - R)
-            if u >= HELP_FROM and u % HELP == 2 and left[0] < ready:
-                leave_next(True)
             negated_max(2 * u)
             if u >= 2:
                 unload_pair(u - 2)
@@ -287,8 +286,11 @@ def tile_hopfieldlayer_pa_t_kernel(tc, x, patterns, out):
                 gram_done += 1
             exponentials(2 * u - 2)
             logits(2 * u + 2)
-            if left[0] < ready:
-                leave_next(False)
+            leave_and_refill(False)
+            if extra(u - 1):
+                leave_and_refill(False)
+            if extra(u):
+                leave_and_refill(True)
 
             negated_max(2 * u + 1)
             if u >= 2:
@@ -298,73 +300,69 @@ def tile_hopfieldlayer_pa_t_kernel(tc, x, patterns, out):
             exponentials(2 * u - 1)
             flip_pair(u - 1)
             logits(2 * u + 3)
-            if left[0] < ready:
-                leave_next(False)
+            if not extra(u):
+                leave_and_refill(False)
             if u % 4 == 0 and 0 < (u + 4) // 4 < NB // 2:
                 flip_x((u + 4) // 4)
 
-        in_tail.append(1)
-        lent = []
-        normal = [issued[0] - 2, issued[0] - 1]
-        gone = [0]
-        quantised = [2 * (NQ - 3)]
-        def more():
+        took_logit_bank, took_product_bank = [], [issued[0] - 2, issued[0] - 1]
+        logits_gone = [0]
+        quantised = [NT - 6]
+
+        def issue():
             while issued[0] < quantised[0]:
-                k = len(lent)
-                if (k < gone[0]) if k < 4 else lent[k - 4] < left[0]:
-                    lent.append(issued[0])
-                    products(1, True)
-                elif normal[-2] < left[0]:
-                    normal.append(issued[0])
-                    products(1)
+                k = len(took_logit_bank)
+                if k < LOGIT_BANKS:
+                    logit_bank_free = k < logits_gone[0]
                 else:
+                    logit_bank_free = took_logit_bank[k - LOGIT_BANKS] < left[0]
+                if not logit_bank_free and took_product_bank[-2] >= left[0]:
                     return
-        def E(m):
+                if logit_bank_free:
+                    took_logit_bank.append(issued[0])
+                else:
+                    took_product_bank.append(issued[0])
+                products(1, logit_bank_free)
+
+        def last_exponentials(m, turn):
             exponentials(m)
-            gone[0] += 1
-            more()
-        def X(m):
-            exponentials(m)
-            flip_tile(m)
-            gone[0] += 1
-            more()
-        def lv(v):
-            if left[0] < issued[0]:
-                leave_next(v)
-            more()
-        def Q(q):
-            quantise_pair(q)
-            quantised[0] += 2
-            more()
-        def QT(m):
-            quantise(m // F, m % F, m % F + 1)
-            quantised[0] += 1
-            more()
+            if turn:
+                flip_tile(m)
+            logits_gone[0] += 1
+            issue()
+
+        def last_leave(on_vector):
+            leave_next(on_vector)
+            issue()
+
+        def last_quantise(m0, m1):
+            quantise(m0 // F, m0 % F, m0 % F + m1 - m0)
+            quantised[0] = m1
+            issue()
 
         negated_max(NT - 2)
-        E(NT - 4)
-        lv(False)
+        last_exponentials(NT - 4, False)
+        last_leave(False)
         negated_max(NT - 1)
-        E(NT - 3)
+        last_exponentials(NT - 3, False)
         flip_pair(NQ - 2)
-        lv(False)
+        last_leave(False)
         unload_pair(NQ - 3)
-        X(NT - 2)
-        lv(True)
-        Q(NQ - 3)
-        lv(False)
-        lv(True)
+        last_exponentials(NT - 2, True)
+        last_leave(True)
+        last_quantise(NT - 6, NT - 4)
+        last_leave(False)
+        last_leave(True)
         unload_pair(NQ - 2)
-        X(NT - 1)
-        lv(False)
+        last_exponentials(NT - 1, True)
+        last_leave(False)
         unload_tile(NT - 2)
-        Q(NQ - 2)
-        QT(NT - 2)
-        lv(False)
+        last_quantise(NT - 4, NT - 2)
+        last_quantise(NT - 2, NT - 1)
+        last_leave(False)
         unload_tile(NT - 1)
-        QT(NT - 1)
-        v = False
+        last_quantise(NT - 1, NT)
+        on_vector = True
         while left[0] < NT:
-            lv(v)
-            v = not v
-        assert left[0] == NT, left[0]
+            last_leave(on_vector)
+            on_vector = not on_vector

from contextlib import ExitStack

import concourse.mybir as mybir
from concourse.masks import make_identity

F32 = mybir.dt.float32
BF16 = mybir.dt.bfloat16
U32 = mybir.dt.uint32
U8 = mybir.dt.uint8
FP8X4 = mybir.dt.float8_e4m3fn_x4
ACT = mybir.ActivationFunctionType
ALU = mybir.AluOpType
AX = mybir.AxisListType

P = 128
B, F, C, N = 2048, 4, 512, 128
T = C // P
PB = P // T
NB = B // P
NT = NB * F
NQ = NT // 2
NG = F * T
LAST_PAIRS = 4
FIRST_EXTRA = 13
EVERY = 4
WARM = 4
LOGIT_BANKS = 4
LENT = 2
FLOPS = 2 * (B * F * C * N + F * C * C * N + B * F * C * C)


def tile_hopfieldlayer_pa_t_kernel(tc, x, patterns, out):
    nc = tc.nc
    with ExitStack() as ctx:
        ctx.enter_context(tc.manual_schedule())
        keep = ctx.enter_context(tc.tile_pool(name="keep", bufs=1))
        work = ctx.enter_context(tc.tile_pool(name="work", bufs=3))
        small = ctx.enter_context(tc.tile_pool(name="small", bufs=NQ))
        results = ctx.enter_context(tc.tile_pool(name="results", bufs=NQ))
        logit_banks = ctx.enter_context(tc.psum_pool(name="logit_banks", bufs=LOGIT_BANKS))
        flip_banks = ctx.enter_context(tc.psum_pool(name="flip_banks", bufs=2))
        product_banks = ctx.enter_context(tc.psum_pool(name="product_banks", bufs=2))

        x_v = x.rearrange("(i p) f n -> p i (f n)", i=NB)
        p_v = patterns.rearrange("f (p t) n -> p f t n", t=T)
        out_v = out.rearrange("(i p) f c -> p i f c", i=NB)

        p_sb = keep.tile([P, F, T, N], BF16)
        x_sb = keep.tile([P, NB, F * N], BF16)
        nc.sync.dma_start(out=p_sb[:, 0:1], in_=p_v[:, 0:1])
        nc.sync.dma_start(out=x_sb[:, 0:1, :], in_=x_v[:, 0:1, :])
        nc.sync.dma_start(out=p_sb[:, 1:2], in_=p_v[:, 1:2])
        nc.sync.dma_start(out=x_sb[:, 1:2, :], in_=x_v[:, 1:2, :])
        nc.sync.dma_start(out=p_sb[:, 2:4], in_=p_v[:, 2:4])
        nc.sync.dma_start(out=x_sb[:, 2:4, :], in_=x_v[:, 2:4, :])
        for i0 in (4, 8, 12):
            nc.sync.dma_start(out=x_sb[:, i0 : i0 + 4, :], in_=x_v[:, i0 : i0 + 4, :])

        ident = keep.tile([P, P], BF16)
        make_identity(nc, ident[:])
        ident_words = keep.tile([P, P], F32)
        make_identity(nc, ident_words[:])
        one_column = keep.tile([P, 1], F32)
        unused = keep.tile([P, 1], F32)
        nc.vector.memset(one_column[:], 0.0)
        nc.scalar.activation(out=unused[:], in_=one_column[:], func=ACT.Exp)
        zeros = keep.tile([P, C], BF16)
        nc.vector.memset(zeros[:], 0.0)
        idle = logit_banks.tile([P, C], F32, tag="bank", name="idle")
        for r in range(WARM):
            nc.tensor.matmul(out=idle[:], lhsT=zeros[:, 0:P], rhs=zeros[:], start=True, stop=True)

        pt = keep.tile([P, F, C], BF16)
        xt = keep.tile([P, NB, F, P], BF16)
        gram_words = keep.tile([P, F, C], U32, align_bytes=64)
        gram_scales = keep.tile([P, F, C], U8, align_bytes=64)

        def flip(n, blocks, pool):
            bank = pool.tile([P, n, P], BF16, tag="bank", name="flipped")
            for r in range(n):
                nc.tensor.transpose(out=bank[:, r, :], in_=blocks(r), identity=ident[:])
            return bank

        xt_ps, s_ps, neg_max, sums, e_sb, et_ps, grouped = {}, {}, {}, {}, {}, {}, {}
        words, scales, inv_sums, y_ps, o_sb, gram_grouped = {}, {}, {}, {}, {}, {}

        def flip_x(h):
            xt_ps[h] = flip(2 * F, lambda r: x_sb[:, 2 * h + r // F, (r % F) * N : (r % F + 1) * N], flip_banks)

        def unload_x(h):
            nc.vector.tensor_copy(out=xt[:, 2 * h : 2 * h + 2].rearrange("n i f p -> n (i f) p"), in_=xt_ps[h][:])

        def copy_x(i, pool, on_vector):
            bank = flip(F, lambda r: x_sb[:, i, r * N : (r + 1) * N], pool)
            if on_vector:
                nc.vector.tensor_copy(out=xt[:, i], in_=bank[:])
            else:
                nc.scalar.copy(out=xt[:, i], in_=bank[:])

        def flip_patterns(f0, f1, pool):
            bank = flip(T * (f1 - f0), lambda r: p_sb[:, f0 + r // T, r % T, :], pool)
            nc.vector.tensor_copy(out=pt[:, f0:f1, :].rearrange("n f (t p) -> n (f t) p", p=P), in_=bank[:])

        def logits(m):
            s_ps[m] = logit_banks.tile([P, C], F32, tag="bank", name="s")
            nc.tensor.matmul(out=s_ps[m][:], lhsT=xt[:, m // F, m % F, :], rhs=pt[:, m % F, :], start=True, stop=True)

        def negated_max(m):
            q, j = m // 2, m % 2
            if j == 0:
                neg_max[q] = small.tile([P, 2], F32, tag="neg_max", name="neg_max")
            nc.vector.tensor_reduce(out=neg_max[q][:, j : j + 1], in_=s_ps[m][:], axis=AX.X, op=ALU.max, negate=True)

        def exponentials(m):
            q, j = m // 2, m % 2
            if j == 0:
                e_sb[q] = work.tile([P, 2, C], BF16, tag="e", name="e")
            if m % F == 0:
                sums[m // F] = small.tile([P, F], F32, tag="sums", name="sums")
            nc.scalar.activation(
                out=e_sb[q][:, j, :].rearrange("b (w p h) -> b w p h", w=2, h=2),
                in_=s_ps[m][:].rearrange("b (w h p) -> b w p h", w=2, h=2),
                func=ACT.Exp,
                bias=neg_max[q][:, j : j + 1],
                scale=1.0,
                accum_out=sums[m // F][:, m % F : m % F + 1],
            )

        def flip_tile(m):
            q, j = m // 2, m % 2
            et_ps[m, 0] = flip_banks.tile([P, 2, P], F32, tag="bank", name="flipped_tile")
            e_words = e_sb[q][:, j, :].bitcast(F32)
            for w in range(2):
                nc.tensor.transpose(out=et_ps[m, 0][:, w, :], in_=e_words[:, w * P : (w + 1) * P], identity=ident_words[:])

        def unload_tile(m):
            nc.vector.tensor_copy(
                out=grouped[m // F][:, m % F].bitcast(F32), in_=et_ps[m, 0][:].rearrange("p w b -> p b w")
            )

        def flip_pair(q):
            et_ps[q] = flip_banks.tile([P, 2, 2, P], F32, tag="bank", name="flipped_words")
            for j in range(2):
                e_words = e_sb[q][:, j, :].bitcast(F32)
                for w in range(2):
                    nc.tensor.transpose(
                        out=et_ps[q][:, j, w, :], in_=e_words[:, w * P : (w + 1) * P], identity=ident_words[:]
                    )

        def unload_pair(q):
            i, f0 = q // 2, 2 * (q % 2)
            if f0 == 0:
                grouped[i] = work.tile([P, F, P, T], BF16, tag="grouped", name="grouped", align_bytes=64)
            nc.vector.tensor_copy(
                out=grouped[i][:, f0 : f0 + 2].bitcast(F32), in_=et_ps[q][:].rearrange("p j w b -> p j b w")
            )

        def quantise(i, f0, f1):
            if f0 == 0:
                words[i] = work.tile([P, F * P], U32, tag="words", name="words", align_bytes=64, bufs=4)
                scales[i] = work.tile([P, F * P], U8, tag="scales", name="scales", align_bytes=64, bufs=4)
                inv_sums[i] = small.tile([P, F], F32, tag="inv_sums", name="inv_sums")
            nc.vector.reciprocal(out=inv_sums[i][:, f0:f1], in_=sums[i][:, f0:f1])
            nc.vector.quantize_mx(
                out=words[i][:, f0 * P : f1 * P].bitcast(FP8X4),
                scales=scales[i][:, f0 * P : f1 * P],
                in_=grouped[i][:, f0:f1].rearrange("p f b t -> p (f b t)"),
            )

        def quantise_pair(q):
            if q >= NQ - LAST_PAIRS:
                quantise(q // 2, 2 * (q % 2), 2 * (q % 2) + 2)
            elif q % 2 == 1:
                quantise(q // 2, 0, F)

        def product(m, lent):
            if lent:
                y_ps[m] = logit_banks.tile([P, C], F32, tag="bank", name="y")
            else:
                y_ps[m] = product_banks.tile([P, C], F32, tag="bank", name="y")
            if m >= 0:
                i, f = m // F, m % F
                nc.tensor.matmul_mx(
                    out=y_ps[m][:],
                    lhsT=words[i][:, f * P : (f + 1) * P].bitcast(FP8X4),
                    lhsT_scale=scales[i][:, f * P : (f + 1) * P],
                    rhs=gram_words[:, f, :].bitcast(FP8X4),
                    rhs_scale=gram_scales[:, f, :],
                    start=True,
                    stop=True,
                )
            else:
                f, cb = (m + NG) // T, (m + NG) % T
                columns = pt[:, f, :].rearrange("n (s m) -> n s m", s=T)[:, :, cb * PB : (cb + 1) * PB]
                for t in range(T):
                    nc.tensor.matmul(
                        out=y_ps[m][:, t * P : (t + 1) * P].rearrange("p (s m) -> p s m", s=T),
                        lhsT=pt[:, f, t * P : (t + 1) * P],
                        rhs=columns,
                        start=True,
                        stop=True,
                    )

        issued = [-NG]

        def products(n, lent=False):
            for r in range(n):
                product(issued[0], lent)
                issued[0] += 1

        def leave(m, on_vector):
            if m >= 0:
                q, j = m // 2, m % 2
                if j == 0:
                    o_sb[q] = results.tile([P, 2, C], F32, tag="o", name="o")
                dst, src, factor = o_sb[q][:, j, :], y_ps[m][:], inv_sums[m // F][:, m % F : m % F + 1]
                if on_vector:
                    nc.vector.tensor_scalar_mul(out=dst, in0=src, scalar1=factor)
                else:
                    nc.scalar.activation(out=dst, in_=src, func=ACT.Copy, scale=factor)
            else:
                f, cb = (m + NG) // T, (m + NG) % T
                if cb == 0:
                    gram_grouped[f] = work.tile([P, C, T], BF16, tag="gram", name="gram", align_bytes=64, bufs=2)
                dst = gram_grouped[f][:, cb * P : (cb + 1) * P, :].rearrange("p (m s) t -> p m s t", s=T)
                src = y_ps[m][:].rearrange("p (t s m) -> p m s t", t=T, s=T)
                if on_vector:
                    nc.vector.tensor_copy(out=dst, in_=src)
                else:
                    nc.scalar.copy(out=dst, in_=src)

        def quantise_gram(f):
            nc.vector.quantize_mx(
                out=gram_words[:, f, :].bitcast(FP8X4),
                scales=gram_scales[:, f, :],
                in_=gram_grouped[f][:].rearrange("p c t -> p (c t)"),
            )

        def store(q):
            nc.sync.dma_start(out=out_v[:, q // 2, 2 * (q % 2) : 2 * (q % 2) + 2, :], in_=o_sb[q][:])

        left = [-NG]

        def leave_next(on_vector):
            m = left[0]
            left[0] += 1
            leave(m, on_vector)
            if m > 0 and m % 2 == 1:
                store(m // 2)

        def leave_and_refill(on_vector):
            leave_next(on_vector)
            if left[0] > LENT - NG:
                products(1)

        flip_patterns(0, 1, flip_banks)
        copy_x(0, flip_banks, on_vector=False)
        flip_patterns(1, 2, logit_banks)
        copy_x(1, product_banks, on_vector=True)
        products(LENT, True)
        logits(0)
        logits(1)
        products(2)
        leave_and_refill(False)
        leave_and_refill(False)
        negated_max(0)
        negated_max(1)
        flip_patterns(2, 4, flip_banks)
        leave_and_refill(False)
        leave_and_refill(False)
        logits(2)
        logits(3)
        quantise_gram(0)
        flip_x(1)
        gram_done = 1

        def extra(u):
            return u >= FIRST_EXTRA and (u - FIRST_EXTRA) % EVERY == 0

        for u in range(1, NQ - 1):
            negated_max(2 * u)
            if u >= 2:
                unload_pair(u - 2)
            if gram_done < F and left[0] >= (gram_done + 1) * T - NG:
                quantise_gram(gram_done)
                gram_done += 1
            exponentials(2 * u - 2)
            logits(2 * u + 2)
            leave_and_refill(False)
            if extra(u - 1):
                leave_and_refill(False)
            if extra(u):
                leave_and_refill(True)

            negated_max(2 * u + 1)
            if u >= 2:
                quantise_pair(u - 2)
            if u % 4 == 1 and 0 < (u + 3) // 4 < NB // 2:
                unload_x((u + 3) // 4)
            exponentials(2 * u - 1)
            flip_pair(u - 1)
            logits(2 * u + 3)
            if not extra(u):
                leave_and_refill(False)
            if u % 4 == 0 and 0 < (u + 4) // 4 < NB // 2:
                flip_x((u + 4) // 4)

        took_logit_bank, took_product_bank = [], [issued[0] - 2, issued[0] - 1]
        logits_gone = [0]
        quantised = [NT - 6]

        def issue():
            while issued[0] < quantised[0]:
                k = len(took_logit_bank)
                if k < LOGIT_BANKS:
                    logit_bank_free = k < logits_gone[0]
                else:
                    logit_bank_free = took_logit_bank[k - LOGIT_BANKS] < left[0]
                if not logit_bank_free and took_product_bank[-2] >= left[0]:
                    return
                if logit_bank_free:
                    took_logit_bank.append(issued[0])
                else:
                    took_product_bank.append(issued[0])
                products(1, logit_bank_free)

        def last_exponentials(m, turn):
            exponentials(m)
            if turn:
                flip_tile(m)
            logits_gone[0] += 1
            issue()

        def last_leave(on_vector):
            leave_next(on_vector)
            issue()

        def last_quantise(m0, m1):
            quantise(m0 // F, m0 % F, m0 % F + m1 - m0)
            quantised[0] = m1
            issue()

        negated_max(NT - 2)
        last_exponentials(NT - 4, False)
        last_leave(False)
        negated_max(NT - 1)
        last_exponentials(NT - 3, False)
        flip_pair(NQ - 2)
        last_leave(False)
        unload_pair(NQ - 3)
        last_exponentials(NT - 2, True)
        last_leave(True)
        last_quantise(NT - 6, NT - 4)
        last_leave(False)
        last_leave(True)
        unload_pair(NQ - 2)
        last_exponentials(NT - 1, True)
        last_leave(False)
        unload_tile(NT - 2)
        last_quantise(NT - 4, NT - 2)
        last_quantise(NT - 2, NT - 1)
        last_leave(False)
        unload_tile(NT - 1)
        last_quantise(NT - 1, NT)
        on_vector = True
        while left[0] < NT:
            last_leave(on_vector)
            on_vector = not on_vector
